import numpy as np
import ml_dtypes


def mxq(x, axis, fmt="e4m3"):
    dtype, down = {"e4m3": (ml_dtypes.float8_e4m3fn, 7), "e5m2": (ml_dtypes.float8_e5m2, 14)}[fmt]
    v = np.moveaxis(np.asarray(x, np.float32).astype(ml_dtypes.bfloat16).astype(np.float64), axis, -1)
    blocks = v.reshape(v.shape[:-1] + (-1, 32))
    amax = np.abs(blocks).max(-1, keepdims=True)
    byte = np.maximum(np.where(amax > 0, np.frexp(amax)[1] - 1 + 127, 0) - down, 1)
    scale = np.exp2(byte - 127.0)
    codes = (blocks / scale).astype(np.float32).astype(dtype).astype(np.float64)
    return np.moveaxis((codes * scale).reshape(v.shape), -1, axis)


WIDE = False


def mx_kscale(k):
    if not WIDE:
        return np.ones(k)
    levels = np.array([10, -10, 5, -5, 0])
    a = np.random.permutation(np.resize(levels, k // 512 * 4)).reshape(k // 512, 4)
    idx = np.arange(k)
    return np.exp2(a[idx // 512, idx % 128 // 32])


BF16 = ml_dtypes.bfloat16


def bf(x):
    return np.asarray(x, np.float32).astype(BF16)


def f64(x):
    return np.asarray(x).astype(np.float64)


B, HD, NH, H, W, F = 2, 512, 4, 32, 64, 2048
HEAD = HD // NH
P = H * W


def rms_in(x, w, eps=1e-8):
    std = np.std(x, axis=(-2, -1), keepdims=True, ddof=1)
    return x / (std + eps) * w[None, :, None, None]


def setup_inputs():
    n = np.random.standard_normal
    s = mx_kscale(HD)

    def stream():
        return n((B, NH, H, W, HEAD)) * 0.35 * (0.5 + np.random.random((B, NH, 1, 1, HEAD))) + 0.5 * n((B, NH, 1, 1, HEAD))

    return {"xx": bf(stream()), "xy": bf(stream()),
            "x": bf(n((B, HD, H, W)) * (0.5 + np.random.random((B, HD, 1, 1))) + 0.5 * n((B, HD, 1, 1))),
            "norm2_w": bf((1.0 + 0.1 * n(HD)) * s),
            "out_w": bf(n((HD, HD)) / np.sqrt(HD) / s[None, :]),
            "out_b": bf(0.1 * n(HD)),
            "gamma_att": bf(0.5 + 0.2 * n(HD))}


def reference(xx, xy, x, norm2_w, out_w, out_b, gamma_att):
    a = (f64(xx) + f64(xy)) * 0.5
    a = a.transpose(0, 1, 4, 2, 3).reshape(B, HD, H, W)
    a = rms_in(a, f64(norm2_w)).reshape(B, HD, P)
    a = (mxq(f64(out_w), 1, "e4m3") @ mxq(a, 1, "e4m3")) + f64(out_b)[None, :, None]
    return a.reshape(B, HD, H, W) * f64(gamma_att)[None, :, None, None] + f64(x)

@@ -1,0 +1,190 @@
+from contextlib import ExitStack
+
+import concourse.mybir as mybir
+from concourse.masks import make_identity
+
+F32 = mybir.dt.float32
+BF16 = mybir.dt.bfloat16
+U32 = mybir.dt.uint32
+U8 = mybir.dt.uint8
+FP8X4 = mybir.dt.float8_e4m3fn_x4
+ALU = mybir.AluOpType
+ACT = mybir.ActivationFunctionType
+AX = mybir.AxisListType
+
+P = 128
+B = 2
+NH = 4
+HEAD = 128
+HD = NH * HEAD
+POS = 32 * 64
+T = POS // P
+GROUP = 4
+GROUPS = T // GROUP
+CHUNK = 512
+CHUNKS = POS // CHUNK
+OT = HD // P
+EPS = 1e-8
+
+FLOPS = 2 * B * HD * HD * POS
+
+
+def tile_axialattentionblock_pb_t_kernel(tc, xx, xy, x, norm2_w, out_w, out_b, gamma_att, out):
+    nc = tc.nc
+    xx_v = xx.rearrange("b n h (wq t) c -> b n (h wq) t c", t=T)
+    xy_v = xy.rearrange("b n h (wq t) c -> b n (h wq) t c", t=T)
+    x_v = x.rearrange("b (m p) h w -> b m p (h w)", p=P)
+    out_v = out.rearrange("b (m p) h w -> b m p (h w)", p=P)
+
+    with ExitStack() as ctx:
+        const = ctx.enter_context(tc.tile_pool(name="const", bufs=1))
+        stream = ctx.enter_context(tc.tile_pool(name="stream", bufs=3))
+        xpool = ctx.enter_context(tc.tile_pool(name="xpool", bufs=B * OT))
+        respool = ctx.enter_context(tc.tile_pool(name="respool", bufs=1))
+        sums_pool = ctx.enter_context(tc.tile_pool(name="sums", bufs=2))
+        big = ctx.enter_context(tc.tile_pool(name="big", bufs=2))
+        work = ctx.enter_context(tc.tile_pool(name="work", bufs=2))
+        flip = ctx.enter_context(tc.tile_pool(name="flip", bufs=4))
+        psum_t = ctx.enter_context(tc.psum_pool(name="psum_t", bufs=2))
+        psum_acc = ctx.enter_context(tc.psum_pool(name="psum_acc", bufs=4))
+
+        ident = const.tile([P, P], BF16)
+        make_identity(nc, ident[:])
+
+        one = const.tile([P, 1], F32)
+        nc.vector.memset(one[:], 1.0)
+        one_root = const.tile([P, 1], F32)
+        nc.scalar.activation(out=one_root[:], in_=one[:], func=ACT.Sqrt)
+
+        vec_rows = const.tile([P, P], BF16)
+        nc.vector.memset(vec_rows[:], 0.0)
+        nc.sync.dma_start(out=vec_rows[0:NH, :], in_=norm2_w.rearrange("(n c) -> n c", c=HEAD))
+        nc.sync.dma_start(out=vec_rows[NH : 2 * NH, :], in_=out_b.rearrange("(n c) -> n c", c=HEAD))
+        nc.sync.dma_start(out=vec_rows[2 * NH : 3 * NH, :], in_=gamma_att.rearrange("(n c) -> n c", c=HEAD))
+        w_rows = const.tile([P, OT, HD], BF16)
+        nc.sync.dma_start(out=w_rows[:], in_=out_w.rearrange("(m p) j -> p m j", p=P))
+
+        vec_ps = psum_t.tile([P, P], BF16, tag="xxT")
+        nc.tensor.transpose(vec_ps[:], vec_rows[:], ident[:])
+        vecs = const.tile([P, 3 * NH], F32)
+        nc.vector.tensor_copy(out=vecs[:], in_=vec_ps[:, 0 : 3 * NH])
+        gamma = vecs[:, 2 * NH : 3 * NH]
+        half_w = const.tile([P, NH], F32)
+        nc.vector.tensor_scalar_mul(out=half_w[:], in0=vecs[:, 0:NH], scalar1=0.5)
+        bias_gamma = const.tile([P, OT], F32)
+        nc.vector.tensor_tensor(out=bias_gamma[:], in0=vecs[:, NH : 2 * NH], in1=gamma, op=ALU.mult)
+
+        w_grouped = const.tile([P, OT, P, NH], BF16, align_bytes=64)
+        for m in range(OT):
+            wT = psum_t.tile([P, NH, P], BF16, tag="xyT")
+            for t in range(NH):
+                nc.tensor.transpose(wT[:, t, :], w_rows[:, m, t * HEAD : (t + 1) * HEAD], ident[:])
+            nc.vector.tensor_copy(out=w_grouped[:, m], in_=wT[:].rearrange("k t o -> k o t"))
+        w_codes = const.tile([P, HD], U32, align_bytes=64)
+        w_scales = const.tile([P, HD], U8, align_bytes=64)
+        nc.vector.quantize_mx(
+            out=w_codes[:].bitcast(FP8X4),
+            scales=w_scales[:],
+            in_=w_grouped[:].rearrange("k m o t -> k (m o t)"),
+        )
+
+        sT_of = []
+        r_of = []
+        for b in range(B):
+            sT = big.tile([P, NH, POS], F32, tag="sT")
+            sums = sums_pool.tile([P, NH, GROUPS], F32, tag="sums")
+            sumsq = sums_pool.tile([P, NH], F32, tag="sumsq")
+            for n in range(NH):
+                xx_sb = stream.tile([P, T, HEAD], BF16, tag="xx")
+                nc.sync.dma_start(out=xx_sb[:], in_=xx_v[b, n])
+                xy_sb = stream.tile([P, T, HEAD], BF16, tag="xy")
+                nc.sync.dma_start(out=xy_sb[:], in_=xy_v[b, n])
+                s_by_t = sT[:, n, :].rearrange("c (p t) -> c p t", t=T)
+                for g in range(GROUPS):
+                    xyT = psum_t.tile([P, GROUP, P], BF16, tag="xyT")
+                    xxT = psum_t.tile([P, GROUP, P], BF16, tag="xxT")
+                    for i in range(GROUP):
+                        nc.tensor.transpose(xyT[:, i, :], xy_sb[:, g * GROUP + i, :], ident[:])
+                    for i in range(GROUP):
+                        nc.tensor.transpose(xxT[:, i, :], xx_sb[:, g * GROUP + i, :], ident[:])
+                    xyT_sb = flip.tile([P, GROUP, P], BF16, tag="xyT_sb")
+                    nc.scalar.copy(out=xyT_sb[:], in_=xyT[:])
+                    nc.vector.scalar_tensor_tensor(
+                        out=s_by_t[:, :, g * GROUP : (g + 1) * GROUP],
+                        in0=xxT[:].rearrange("c i p -> c p i"),
+                        scalar=1.0,
+                        in1=xyT_sb[:].rearrange("c i p -> c p i"),
+                        op0=ALU.mult,
+                        op1=ALU.add,
+                        accum_out=sums[:, n, g : g + 1],
+                    )
+                squares = work.tile([P, POS], BF16, tag="squares")
+                nc.scalar.activation(out=squares[:], in_=sT[:, n, :], func=ACT.Square, accum_out=sumsq[:, n : n + 1])
+
+            sum_s = sums_pool.tile([P, NH], F32, tag="sum_s")
+            nc.vector.tensor_reduce(out=sum_s[:], in_=sums[:], axis=AX.X, op=ALU.add)
+            sum_s2 = sums_pool.tile([P, NH], F32, tag="sum_s2")
+            nc.vector.tensor_tensor(out=sum_s2[:], in0=sum_s[:], in1=sum_s[:], op=ALU.mult)
+            centred = sums_pool.tile([P, NH], F32, tag="centred")
+            nc.vector.scalar_tensor_tensor(
+                out=centred[:], in0=sum_s2[:], scalar=-1.0 / POS, in1=sumsq[:], op0=ALU.mult, op1=ALU.add
+            )
+            var = sums_pool.tile([P, NH], F32, tag="var")
+            nc.vector.tensor_scalar(
+                out=var[:], in0=centred[:], scalar1=0.25 / (POS - 1), scalar2=0.0, op0=ALU.mult, op1=ALU.max
+            )
+            std = sums_pool.tile([P, NH], F32, tag="std")
+            nc.scalar.activation(out=std[:], in_=var[:], func=ACT.Sqrt)
+            den = sums_pool.tile([P, NH], F32, tag="den")
+            nc.vector.tensor_scalar_add(out=den[:], in0=std[:], scalar1=EPS)
+            inv = sums_pool.tile([P, NH], F32, tag="inv")
+            nc.vector.reciprocal(out=inv[:], in_=den[:])
+            r = sums_pool.tile([P, NH], F32, tag="r")
+            nc.vector.tensor_tensor(out=r[:], in0=inv[:], in1=half_w[:], op=ALU.mult)
+            sT_of.append(sT)
+            r_of.append(r)
+
+        res_of = {}
+        for b in range(B):
+            for m in range(OT):
+                x_sb = xpool.tile([P, POS], BF16, tag="x")
+                nc.sync.dma_start(out=x_sb[:], in_=x_v[b, m])
+                res = respool.tile([P, POS], F32, name="res%d%d" % (b, m))
+                nc.gpsimd.tensor_scalar(
+                    out=res[:], in0=x_sb[:], scalar1=1.0, scalar2=bias_gamma[:, m : m + 1], op0=ALU.mult, op1=ALU.add
+                )
+                res_of[(b, m)] = res
+
+        for b in range(B):
+            for q in range(CHUNKS):
+                cols = slice(q * CHUNK, (q + 1) * CHUNK)
+                grouped = work.tile([P, CHUNK, NH], BF16, tag="grouped", align_bytes=64)
+                nc.vector.tensor_tensor(
+                    out=grouped[:],
+                    in0=sT_of[b][:, :, cols].rearrange("c n p -> c p n"),
+                    in1=r_of[b][:].unsqueeze(1).to_broadcast([P, CHUNK, NH]),
+                    op=ALU.mult,
+                )
+                g_codes = work.tile([P, CHUNK], U32, tag="g_codes", align_bytes=64)
+                g_scales = work.tile([P, CHUNK], U8, tag="g_scales", align_bytes=64)
+                nc.vector.quantize_mx(
+                    out=g_codes[:].bitcast(FP8X4),
+                    scales=g_scales[:],
+                    in_=grouped[:].rearrange("c p n -> c (p n)"),
+                )
+                for m in range(OT):
+                    acc = psum_acc.tile([P, CHUNK], F32, tag="acc")
+                    nc.tensor.matmul_mx(
+                        out=acc[:],
+                        lhsT=w_codes[:, m * P : (m + 1) * P].bitcast(FP8X4),
+                        lhsT_scale=w_scales[:, m * P : (m + 1) * P],
+                        rhs=g_codes[:].bitcast(FP8X4),
+                        rhs_scale=g_scales[:],
+                        start=True,
+                        stop=True,
+                    )
+                    res = res_of[(b, m)]
+                    nc.vector.scalar_tensor_tensor(
+                        out=res[:, cols], in0=acc[:], scalar=gamma[:, m : m + 1], in1=res[:, cols], op0=ALU.mult, op1=ALU.add
+                    )
+                    nc.sync.dma_start(out=out_v[b, m][:, cols], in_=res[:, cols])

@@ -21,9 +21,11 @@ POS = 32 * 64
 T = POS // P
 GROUP = 4
 GROUPS = T // GROUP
-CHUNK = 512
-CHUNKS = POS // CHUNK
+CHUNK = GROUP * P
 OT = HD // P
+VECTOR_TILES = (0, 2)
+SCALAR_TILES = (1, 3)
+R_PAD = 32
 EPS = 1e-8
 
 FLOPS = 2 * B * HD * HD * POS
@@ -41,15 +43,22 @@ def tile_axialattentionblock_pb_t_kernel(tc, xx, xy, x, norm2_w, out_w, out_b, g
         stream = ctx.enter_context(tc.tile_pool(name="stream", bufs=3))
         xpool = ctx.enter_context(tc.tile_pool(name="xpool", bufs=B * OT))
         respool = ctx.enter_context(tc.tile_pool(name="respool", bufs=1))
+        outpool = ctx.enter_context(tc.tile_pool(name="outpool", bufs=3))
         sums_pool = ctx.enter_context(tc.tile_pool(name="sums", bufs=2))
         big = ctx.enter_context(tc.tile_pool(name="big", bufs=2))
+        junk = ctx.enter_context(tc.tile_pool(name="junk", bufs=1))
         work = ctx.enter_context(tc.tile_pool(name="work", bufs=2))
         flip = ctx.enter_context(tc.tile_pool(name="flip", bufs=4))
-        psum_t = ctx.enter_context(tc.psum_pool(name="psum_t", bufs=2))
+        psum_t = ctx.enter_context(tc.psum_pool(name="psum_t", bufs=3))
         psum_acc = ctx.enter_context(tc.psum_pool(name="psum_acc", bufs=4))
+        psum_r = ctx.enter_context(tc.psum_pool(name="psum_r", bufs=1))
 
         ident = const.tile([P, P], BF16)
         make_identity(nc, ident[:])
+        ident32 = const.tile([P, P], F32)
+        make_identity(nc, ident32[:])
+        r_pad = const.tile([P, B, R_PAD], F32)
+        nc.vector.memset(r_pad[:], 0.0)
 
         one = const.tile([P, 1], F32)
         nc.vector.memset(one[:], 1.0)
@@ -64,7 +73,7 @@ def tile_axialattentionblock_pb_t_kernel(tc, xx, xy, x, norm2_w, out_w, out_b, g
         w_rows = const.tile([P, OT, HD], BF16)
         nc.sync.dma_start(out=w_rows[:], in_=out_w.rearrange("(m p) j -> p m j", p=P))
 
-        vec_ps = psum_t.tile([P, P], BF16, tag="xxT")
+        vec_ps = psum_t.tile([P, P], BF16, tag="tr")
         nc.tensor.transpose(vec_ps[:], vec_rows[:], ident[:])
         vecs = const.tile([P, 3 * NH], F32)
         nc.vector.tensor_copy(out=vecs[:], in_=vec_ps[:, 0 : 3 * NH])
@@ -76,7 +85,7 @@ def tile_axialattentionblock_pb_t_kernel(tc, xx, xy, x, norm2_w, out_w, out_b, g
 
         w_grouped = const.tile([P, OT, P, NH], BF16, align_bytes=64)
         for m in range(OT):
-            wT = psum_t.tile([P, NH, P], BF16, tag="xyT")
+            wT = psum_t.tile([P, NH, P], BF16, tag="tr")
             for t in range(NH):
                 nc.tensor.transpose(wT[:, t, :], w_rows[:, m, t * HEAD : (t + 1) * HEAD], ident[:])
             nc.vector.tensor_copy(out=w_grouped[:, m], in_=wT[:].rearrange("k t o -> k o t"))
@@ -89,7 +98,6 @@ def tile_axialattentionblock_pb_t_kernel(tc, xx, xy, x, norm2_w, out_w, out_b, g
         )
 
         sT_of = []
-        r_of = []
         for b in range(B):
             sT = big.tile([P, NH, POS], F32, tag="sT")
             sums = sums_pool.tile([P, NH, GROUPS], F32, tag="sums")
@@ -99,10 +107,9 @@ def tile_axialattentionblock_pb_t_kernel(tc, xx, xy, x, norm2_w, out_w, out_b, g
                 nc.sync.dma_start(out=xx_sb[:], in_=xx_v[b, n])
                 xy_sb = stream.tile([P, T, HEAD], BF16, tag="xy")
                 nc.sync.dma_start(out=xy_sb[:], in_=xy_v[b, n])
-                s_by_t = sT[:, n, :].rearrange("c (p t) -> c p t", t=T)
                 for g in range(GROUPS):
-                    xyT = psum_t.tile([P, GROUP, P], BF16, tag="xyT")
-                    xxT = psum_t.tile([P, GROUP, P], BF16, tag="xxT")
+                    xyT = psum_t.tile([P, GROUP, P], BF16, tag="tr")
+                    xxT = psum_t.tile([P, GROUP, P], BF16, tag="tr")
                     for i in range(GROUP):
                         nc.tensor.transpose(xyT[:, i, :], xy_sb[:, g * GROUP + i, :], ident[:])
                     for i in range(GROUP):
@@ -110,15 +117,15 @@ def tile_axialattentionblock_pb_t_kernel(tc, xx, xy, x, norm2_w, out_w, out_b, g
                     xyT_sb = flip.tile([P, GROUP, P], BF16, tag="xyT_sb")
                     nc.scalar.copy(out=xyT_sb[:], in_=xyT[:])
                     nc.vector.scalar_tensor_tensor(
-                        out=s_by_t[:, :, g * GROUP : (g + 1) * GROUP],
-                        in0=xxT[:].rearrange("c i p -> c p i"),
+                        out=sT[:, n, g * CHUNK : (g + 1) * CHUNK],
+                        in0=xxT[:].rearrange("c i p -> c (i p)"),
                         scalar=1.0,
-                        in1=xyT_sb[:].rearrange("c i p -> c p i"),
+                        in1=xyT_sb[:].rearrange("c i p -> c (i p)"),
                         op0=ALU.mult,
                         op1=ALU.add,
                         accum_out=sums[:, n, g : g + 1],
                     )
-                squares = work.tile([P, POS], BF16, tag="squares")
+                squares = junk.tile([P, POS], BF16, tag="squares")
                 nc.scalar.activation(out=squares[:], in_=sT[:, n, :], func=ACT.Square, accum_out=sumsq[:, n : n + 1])
 
             sum_s = sums_pool.tile([P, NH], F32, tag="sum_s")
@@ -139,52 +146,98 @@ def tile_axialattentionblock_pb_t_kernel(tc, xx, xy, x, norm2_w, out_w, out_b, g
             nc.vector.tensor_scalar_add(out=den[:], in0=std[:], scalar1=EPS)
             inv = sums_pool.tile([P, NH], F32, tag="inv")
             nc.vector.reciprocal(out=inv[:], in_=den[:])
-            r = sums_pool.tile([P, NH], F32, tag="r")
-            nc.vector.tensor_tensor(out=r[:], in0=inv[:], in1=half_w[:], op=ALU.mult)
+            nc.vector.tensor_tensor(out=r_pad[:, b, 0:NH], in0=inv[:], in1=half_w[:], op=ALU.mult)
             sT_of.append(sT)
-            r_of.append(r)
 
+        x_of = {}
         res_of = {}
         for b in range(B):
-            for m in range(OT):
+            for m in SCALAR_TILES + VECTOR_TILES:
                 x_sb = xpool.tile([P, POS], BF16, tag="x")
                 nc.sync.dma_start(out=x_sb[:], in_=x_v[b, m])
+                x_of[(b, m)] = x_sb
+            for m in VECTOR_TILES:
                 res = respool.tile([P, POS], F32, name="res%d%d" % (b, m))
                 nc.gpsimd.tensor_scalar(
-                    out=res[:], in0=x_sb[:], scalar1=1.0, scalar2=bias_gamma[:, m : m + 1], op0=ALU.mult, op1=ALU.add
+                    out=res[:],
+                    in0=x_of[(b, m)][:],
+                    scalar1=1.0,
+                    scalar2=bias_gamma[:, m : m + 1],
+                    op0=ALU.mult,
+                    op1=ALU.add,
                 )
                 res_of[(b, m)] = res
 
+        def project(m, codes, scales):
+            acc = psum_acc.tile([P, CHUNK], F32, tag="acc")
+            nc.tensor.matmul_mx(
+                out=acc[:],
+                lhsT=w_codes[:, m * P : (m + 1) * P].bitcast(FP8X4),
+                lhsT_scale=w_scales[:, m * P : (m + 1) * P],
+                rhs=codes[:].bitcast(FP8X4),
+                rhs_scale=scales[:],
+                start=True,
+                stop=True,
+            )
+            return acc[:].rearrange("o (i p) -> o p i", i=GROUP)
+
+        def positions_of_group(tile_ap, g):
+            return tile_ap.rearrange("o (p t) -> o p t", t=T)[:, :, g * GROUP : (g + 1) * GROUP]
+
         for b in range(B):
-            for q in range(CHUNKS):
-                cols = slice(q * CHUNK, (q + 1) * CHUNK)
+            r_ps = psum_r.tile([P, R_PAD], F32, tag="r")
+            nc.tensor.matmul(out=r_ps[:], lhsT=ident32[:], rhs=r_pad[:, b, :], start=True, stop=True)
+            out_of = {}
+            for m in SCALAR_TILES:
+                out_of[m] = outpool.tile([P, POS], F32, tag="out_sb", name="out_sb%d%d" % (b, m))
+            codes_of = []
+            scales_of = []
+            for g in range(GROUPS):
+                cols = slice(g * CHUNK, (g + 1) * CHUNK)
                 grouped = work.tile([P, CHUNK, NH], BF16, tag="grouped", align_bytes=64)
                 nc.vector.tensor_tensor(
                     out=grouped[:],
                     in0=sT_of[b][:, :, cols].rearrange("c n p -> c p n"),
-                    in1=r_of[b][:].unsqueeze(1).to_broadcast([P, CHUNK, NH]),
+                    in1=r_ps[:, 0:NH].unsqueeze(1).to_broadcast([P, CHUNK, NH]),
                     op=ALU.mult,
                 )
-                g_codes = work.tile([P, CHUNK], U32, tag="g_codes", align_bytes=64)
-                g_scales = work.tile([P, CHUNK], U8, tag="g_scales", align_bytes=64)
+                g_codes = flip.tile([P, CHUNK], U32, tag="g_codes", align_bytes=64)
+                g_scales = flip.tile([P, CHUNK], U8, tag="g_scales", align_bytes=64)
                 nc.vector.quantize_mx(
                     out=g_codes[:].bitcast(FP8X4),
                     scales=g_scales[:],
                     in_=grouped[:].rearrange("c p n -> c (p n)"),
                 )
-                for m in range(OT):
-                    acc = psum_acc.tile([P, CHUNK], F32, tag="acc")
-                    nc.tensor.matmul_mx(
-                        out=acc[:],
-                        lhsT=w_codes[:, m * P : (m + 1) * P].bitcast(FP8X4),
-                        lhsT_scale=w_scales[:, m * P : (m + 1) * P],
-                        rhs=g_codes[:].bitcast(FP8X4),
-                        rhs_scale=g_scales[:],
-                        start=True,
-                        stop=True,
+                codes_of.append(g_codes)
+                scales_of.append(g_scales)
+                for m in SCALAR_TILES:
+                    acc_by_pos = project(m, g_codes, g_scales)
+                    y = flip.tile([P, P, GROUP], F32, tag="y")
+                    nc.scalar.activation(
+                        out=y[:],
+                        in_=acc_by_pos,
+                        func=ACT.Identity,
+                        bias=bias_gamma[:, m : m + 1],
+                        scale=gamma[:, m : m + 1],
                     )
-                    res = res_of[(b, m)]
+                    nc.gpsimd.tensor_tensor(
+                        out=positions_of_group(out_of[m][:], g),
+                        in0=y[:],
+                        in1=positions_of_group(x_of[(b, m)][:], g),
+                        op=ALU.add,
+                    )
+            for m in SCALAR_TILES:
+                nc.sync.dma_start(out=out_v[b, m], in_=out_of[m][:])
+            for m in VECTOR_TILES:
+                res = res_of[(b, m)]
+                for g in range(GROUPS):
+                    acc_by_pos = project(m, codes_of[g], scales_of[g])
                     nc.vector.scalar_tensor_tensor(
-                        out=res[:, cols], in0=acc[:], scalar=gamma[:, m : m + 1], in1=res[:, cols], op0=ALU.mult, op1=ALU.add
+                        out=positions_of_group(res[:], g),
+                        in0=acc_by_pos,
+                        scalar=gamma[:, m : m + 1],
+                        in1=positions_of_group(res[:], g),
+                        op0=ALU.mult,
+                        op1=ALU.add,
                     )
-                    nc.sync.dma_start(out=out_v[b, m][:, cols], in_=res[:, cols])
+                nc.sync.dma_start(out=out_v[b, m], in_=res[:])

@@ -18,40 +18,47 @@ NH = 4
 HEAD = 128
 HD = NH * HEAD
 POS = 32 * 64
-T = POS // P
-GROUP = 4
-GROUPS = T // GROUP
-CHUNK = GROUP * P
+HALVES = 2
+HALF = POS // HALVES
+OCT = HALF // P
+CHUNK = 512
+QUAD = CHUNK // P
+PAIR = OCT // QUAD
+CHUNKS = POS // CHUNK
 OT = HD // P
 VECTOR_TILES = (0, 2)
 SCALAR_TILES = (1, 3)
 R_PAD = 32
+PREFETCH = 4
 EPS = 1e-8
 
 FLOPS = 2 * B * HD * HD * POS
 
+assert CHUNKS == NH
+
 
 def tile_axialattentionblock_pb_t_kernel(tc, xx, xy, x, norm2_w, out_w, out_b, gamma_att, out):
     nc = tc.nc
-    xx_v = xx.rearrange("b n h (wq t) c -> b n (h wq) t c", t=T)
-    xy_v = xy.rearrange("b n h (wq t) c -> b n (h wq) t c", t=T)
+    by_partition = "b n (hh hp) (wp i) c -> b n (hp wp) hh i c"
+    xx_v = xx.rearrange(by_partition, hh=HALVES, i=OCT)
+    xy_v = xy.rearrange(by_partition, hh=HALVES, i=OCT)
     x_v = x.rearrange("b (m p) h w -> b m p (h w)", p=P)
     out_v = out.rearrange("b (m p) h w -> b m p (h w)", p=P)
 
     with ExitStack() as ctx:
         const = ctx.enter_context(tc.tile_pool(name="const", bufs=1))
-        stream = ctx.enter_context(tc.tile_pool(name="stream", bufs=3))
+        stream = ctx.enter_context(tc.tile_pool(name="stream", bufs=PREFETCH))
         xpool = ctx.enter_context(tc.tile_pool(name="xpool", bufs=B * OT))
         respool = ctx.enter_context(tc.tile_pool(name="respool", bufs=1))
-        outpool = ctx.enter_context(tc.tile_pool(name="outpool", bufs=3))
+        ypool = ctx.enter_context(tc.tile_pool(name="ypool", bufs=4))
         sums_pool = ctx.enter_context(tc.tile_pool(name="sums", bufs=2))
         big = ctx.enter_context(tc.tile_pool(name="big", bufs=2))
         junk = ctx.enter_context(tc.tile_pool(name="junk", bufs=1))
-        work = ctx.enter_context(tc.tile_pool(name="work", bufs=2))
-        flip = ctx.enter_context(tc.tile_pool(name="flip", bufs=4))
+        work = ctx.enter_context(tc.tile_pool(name="work", bufs=3))
         psum_t = ctx.enter_context(tc.psum_pool(name="psum_t", bufs=3))
         psum_acc = ctx.enter_context(tc.psum_pool(name="psum_acc", bufs=4))
         psum_r = ctx.enter_context(tc.psum_pool(name="psum_r", bufs=1))
+        ctx.enter_context(tc.manual_schedule())
 
         ident = const.tile([P, P], BF16)
         make_identity(nc, ident[:])
@@ -72,6 +79,19 @@ def tile_axialattentionblock_pb_t_kernel(tc, xx, xy, x, norm2_w, out_w, out_b, g
         nc.sync.dma_start(out=vec_rows[2 * NH : 3 * NH, :], in_=gamma_att.rearrange("(n c) -> n c", c=HEAD))
         w_rows = const.tile([P, OT, HD], BF16)
         nc.sync.dma_start(out=w_rows[:], in_=out_w.rearrange("(m p) j -> p m j", p=P))
+
+        streams_of = {}
+
+        def load_head(u):
+            b, n = divmod(u, NH)
+            xx_sb = stream.tile([P, HALVES, OCT, HEAD], BF16, tag="xx")
+            nc.sync.dma_start(out=xx_sb[:], in_=xx_v[b, n])
+            xy_sb = stream.tile([P, HALVES, OCT, HEAD], BF16, tag="xy")
+            nc.sync.dma_start(out=xy_sb[:], in_=xy_v[b, n])
+            streams_of[u] = (xx_sb, xy_sb)
+
+        for u in range(PREFETCH):
+            load_head(u)
 
         vec_ps = psum_t.tile([P, P], BF16, tag="tr")
         nc.tensor.transpose(vec_ps[:], vec_rows[:], ident[:])
@@ -97,37 +117,62 @@ def tile_axialattentionblock_pb_t_kernel(tc, xx, xy, x, norm2_w, out_w, out_b, g
             in_=w_grouped[:].rearrange("k m o t -> k (m o t)"),
         )
 
-        sT_of = []
-        for b in range(B):
-            sT = big.tile([P, NH, POS], F32, tag="sT")
-            sums = sums_pool.tile([P, NH, GROUPS], F32, tag="sums")
-            sumsq = sums_pool.tile([P, NH], F32, tag="sumsq")
-            for n in range(NH):
-                xx_sb = stream.tile([P, T, HEAD], BF16, tag="xx")
-                nc.sync.dma_start(out=xx_sb[:], in_=xx_v[b, n])
-                xy_sb = stream.tile([P, T, HEAD], BF16, tag="xy")
-                nc.sync.dma_start(out=xy_sb[:], in_=xy_v[b, n])
-                for g in range(GROUPS):
-                    xyT = psum_t.tile([P, GROUP, P], BF16, tag="tr")
-                    xxT = psum_t.tile([P, GROUP, P], BF16, tag="tr")
-                    for i in range(GROUP):
-                        nc.tensor.transpose(xyT[:, i, :], xy_sb[:, g * GROUP + i, :], ident[:])
-                    for i in range(GROUP):
-                        nc.tensor.transpose(xxT[:, i, :], xx_sb[:, g * GROUP + i, :], ident[:])
-                    xyT_sb = flip.tile([P, GROUP, P], BF16, tag="xyT_sb")
-                    nc.scalar.copy(out=xyT_sb[:], in_=xyT[:])
-                    nc.vector.scalar_tensor_tensor(
-                        out=sT[:, n, g * CHUNK : (g + 1) * CHUNK],
-                        in0=xxT[:].rearrange("c i p -> c (i p)"),
-                        scalar=1.0,
-                        in1=xyT_sb[:].rearrange("c i p -> c (i p)"),
-                        op0=ALU.mult,
-                        op1=ALU.add,
-                        accum_out=sums[:, n, g : g + 1],
-                    )
-                squares = junk.tile([P, POS], BF16, tag="squares")
-                nc.scalar.activation(out=squares[:], in_=sT[:, n, :], func=ACT.Square, accum_out=sumsq[:, n : n + 1])
+        sT_of = {}
+        sums_of = {}
+        x_of = {}
+        res_of = {}
+        r_of = {}
+        codes_of = {}
+        y_of = {}
 
+        def sum_head(b, n):
+            u = b * NH + n
+            if n == 0:
+                sT_of[b] = big.tile([P, NH, POS], F32, tag="sT", name="sT%d" % b)
+                sums_of[b] = (
+                    sums_pool.tile([P, NH, HALVES], F32, tag="sums", name="sums%d" % b),
+                    sums_pool.tile([P, NH], F32, tag="sumsq", name="sumsq%d" % b),
+                )
+            xx_sb, xy_sb = streams_of[u]
+            for h in range(HALVES):
+                xyT = psum_t.tile([P, OCT, P], BF16, tag="tr")
+                for i in range(OCT):
+                    nc.tensor.transpose(xyT[:, i, :], xy_sb[:, h, i, :], ident[:])
+                xxT = psum_t.tile([P, OCT, P], BF16, tag="tr")
+                for i in range(OCT):
+                    nc.tensor.transpose(xxT[:, i, :], xx_sb[:, h, i, :], ident[:])
+                xyT_sb = work.tile([P, HALF], BF16, tag="xyT_sb")
+                nc.scalar.copy(out=xyT_sb[:], in_=xyT[:].rearrange("c i p -> c (i p)"))
+                nc.vector.scalar_tensor_tensor(
+                    out=sT_of[b][:, n, h * HALF : (h + 1) * HALF],
+                    in0=xxT[:].rearrange("c i p -> c (i p)"),
+                    scalar=1.0,
+                    in1=xyT_sb[:],
+                    op0=ALU.mult,
+                    op1=ALU.add,
+                    accum_out=sums_of[b][0][:, n, h : h + 1],
+                )
+            if u + PREFETCH < B * NH:
+                load_head(u + PREFETCH)
+            m = n
+            x_sb = xpool.tile([P, POS], BF16, tag="x")
+            nc.sync.dma_start(out=x_sb[:], in_=x_v[b, m])
+            x_of[(b, m)] = x_sb
+            if m in VECTOR_TILES:
+                res = respool.tile([P, POS], F32, name="res%d%d" % (b, m))
+                nc.gpsimd.tensor_scalar(
+                    out=res[:], in0=x_sb[:], scalar1=1.0, scalar2=bias_gamma[:, m : m + 1], op0=ALU.mult, op1=ALU.add
+                )
+                res_of[(b, m)] = res
+
+        def square_head(b, n):
+            squares = junk.tile([P, POS], BF16, tag="squares")
+            nc.scalar.activation(
+                out=squares[:], in_=sT_of[b][:, n, :], func=ACT.Square, accum_out=sums_of[b][1][:, n : n + 1]
+            )
+
+        def scale_factors(b):
+            sums, sumsq = sums_of[b]
             sum_s = sums_pool.tile([P, NH], F32, tag="sum_s")
             nc.vector.tensor_reduce(out=sum_s[:], in_=sums[:], axis=AX.X, op=ALU.add)
             sum_s2 = sums_pool.tile([P, NH], F32, tag="sum_s2")
@@ -147,97 +192,87 @@ def tile_axialattentionblock_pb_t_kernel(tc, xx, xy, x, norm2_w, out_w, out_b, g
             inv = sums_pool.tile([P, NH], F32, tag="inv")
             nc.vector.reciprocal(out=inv[:], in_=den[:])
             nc.vector.tensor_tensor(out=r_pad[:, b, 0:NH], in0=inv[:], in1=half_w[:], op=ALU.mult)
-            sT_of.append(sT)
+            r_ps = psum_r.tile([P, R_PAD], F32, tag="r")
+            nc.tensor.matmul(out=r_ps[:], lhsT=ident32[:], rhs=r_pad[:, b, :], start=True, stop=True)
+            r_of[b] = r_ps
 
-        x_of = {}
-        res_of = {}
-        for b in range(B):
+        def quantise_chunk(b, g):
+            grouped = work.tile([P, CHUNK, NH], BF16, tag="grouped", align_bytes=64)
+            nc.vector.tensor_tensor(
+                out=grouped[:],
+                in0=sT_of[b][:, :, g * CHUNK : (g + 1) * CHUNK].rearrange("c n p -> c p n"),
+                in1=r_of[b][:, 0:NH].unsqueeze(1).to_broadcast([P, CHUNK, NH]),
+                op=ALU.mult,
+            )
+            g_codes = work.tile([P, CHUNK], U32, tag="g_codes", align_bytes=64)
+            g_scales = work.tile([P, CHUNK], U8, tag="g_scales", align_bytes=64)
+            nc.vector.quantize_mx(
+                out=g_codes[:].bitcast(FP8X4),
+                scales=g_scales[:],
+                in_=grouped[:].rearrange("c p n -> c (p n)"),
+            )
+            codes_of[(b, g)] = (g_codes, g_scales)
+
+        def runs_of_chunk(half_ap, k):
+            return half_ap.rearrange("o (p k i) -> o p k i", k=PAIR, i=QUAD)[:, :, k, :]
+
+        def finish_chunk(b, g):
+            h, k = divmod(g, PAIR)
+            half = slice(h * HALF, (h + 1) * HALF)
+            g_codes, g_scales = codes_of[(b, g)]
+            acc_of = {}
             for m in SCALAR_TILES + VECTOR_TILES:
-                x_sb = xpool.tile([P, POS], BF16, tag="x")
-                nc.sync.dma_start(out=x_sb[:], in_=x_v[b, m])
-                x_of[(b, m)] = x_sb
+                acc = psum_acc.tile([P, CHUNK], F32, tag="acc")
+                nc.tensor.matmul_mx(
+                    out=acc[:],
+                    lhsT=w_codes[:, m * P : (m + 1) * P].bitcast(FP8X4),
+                    lhsT_scale=w_scales[:, m * P : (m + 1) * P],
+                    rhs=g_codes[:].bitcast(FP8X4),
+                    rhs_scale=g_scales[:],
+                    start=True,
+                    stop=True,
+                )
+                acc_of[m] = acc[:].rearrange("o (i p) -> o p i", i=QUAD)
+            for m in SCALAR_TILES:
+                if k == 0:
+                    y_of[(b, m)] = ypool.tile([P, HALF], F32, tag="y", name="y%d%d%d" % (b, m, h))
+                y = y_of[(b, m)]
+                nc.scalar.activation(
+                    out=runs_of_chunk(y[:], k),
+                    in_=acc_of[m],
+                    func=ACT.Identity,
+                    bias=bias_gamma[:, m : m + 1],
+                    scale=gamma[:, m : m + 1],
+                )
+                if k == PAIR - 1:
+                    nc.gpsimd.tensor_tensor(out=y[:], in0=y[:], in1=x_of[(b, m)][:, half], op=ALU.add)
+                    nc.sync.dma_start(out=out_v[b, m][:, half], in_=y[:])
             for m in VECTOR_TILES:
-                res = respool.tile([P, POS], F32, name="res%d%d" % (b, m))
-                nc.gpsimd.tensor_scalar(
-                    out=res[:],
-                    in0=x_of[(b, m)][:],
-                    scalar1=1.0,
-                    scalar2=bias_gamma[:, m : m + 1],
+                res = res_of[(b, m)]
+                nc.vector.scalar_tensor_tensor(
+                    out=runs_of_chunk(res[:, half], k),
+                    in0=acc_of[m],
+                    scalar=gamma[:, m : m + 1],
+                    in1=runs_of_chunk(res[:, half], k),
                     op0=ALU.mult,
                     op1=ALU.add,
                 )
-                res_of[(b, m)] = res
+                if k == PAIR - 1:
+                    nc.sync.dma_start(out=out_v[b, m][:, half], in_=res[:, half])
 
-        def project(m, codes, scales):
-            acc = psum_acc.tile([P, CHUNK], F32, tag="acc")
-            nc.tensor.matmul_mx(
-                out=acc[:],
-                lhsT=w_codes[:, m * P : (m + 1) * P].bitcast(FP8X4),
-                lhsT_scale=w_scales[:, m * P : (m + 1) * P],
-                rhs=codes[:].bitcast(FP8X4),
-                rhs_scale=scales[:],
-                start=True,
-                stop=True,
-            )
-            return acc[:].rearrange("o (i p) -> o p i", i=GROUP)
-
-        def positions_of_group(tile_ap, g):
-            return tile_ap.rearrange("o (p t) -> o p t", t=T)[:, :, g * GROUP : (g + 1) * GROUP]
-
-        for b in range(B):
-            r_ps = psum_r.tile([P, R_PAD], F32, tag="r")
-            nc.tensor.matmul(out=r_ps[:], lhsT=ident32[:], rhs=r_pad[:, b, :], start=True, stop=True)
-            out_of = {}
-            for m in SCALAR_TILES:
-                out_of[m] = outpool.tile([P, POS], F32, tag="out_sb", name="out_sb%d%d" % (b, m))
-            codes_of = []
-            scales_of = []
-            for g in range(GROUPS):
-                cols = slice(g * CHUNK, (g + 1) * CHUNK)
-                grouped = work.tile([P, CHUNK, NH], BF16, tag="grouped", align_bytes=64)
-                nc.vector.tensor_tensor(
-                    out=grouped[:],
-                    in0=sT_of[b][:, :, cols].rearrange("c n p -> c p n"),
-                    in1=r_ps[:, 0:NH].unsqueeze(1).to_broadcast([P, CHUNK, NH]),
-                    op=ALU.mult,
-                )
-                g_codes = flip.tile([P, CHUNK], U32, tag="g_codes", align_bytes=64)
-                g_scales = flip.tile([P, CHUNK], U8, tag="g_scales", align_bytes=64)
-                nc.vector.quantize_mx(
-                    out=g_codes[:].bitcast(FP8X4),
-                    scales=g_scales[:],
-                    in_=grouped[:].rearrange("c p n -> c (p n)"),
-                )
-                codes_of.append(g_codes)
-                scales_of.append(g_scales)
-                for m in SCALAR_TILES:
-                    acc_by_pos = project(m, g_codes, g_scales)
-                    y = flip.tile([P, P, GROUP], F32, tag="y")
-                    nc.scalar.activation(
-                        out=y[:],
-                        in_=acc_by_pos,
-                        func=ACT.Identity,
-                        bias=bias_gamma[:, m : m + 1],
-                        scale=gamma[:, m : m + 1],
-                    )
-                    nc.gpsimd.tensor_tensor(
-                        out=positions_of_group(out_of[m][:], g),
-                        in0=y[:],
-                        in1=positions_of_group(x_of[(b, m)][:], g),
-                        op=ALU.add,
-                    )
-            for m in SCALAR_TILES:
-                nc.sync.dma_start(out=out_v[b, m], in_=out_of[m][:])
-            for m in VECTOR_TILES:
-                res = res_of[(b, m)]
-                for g in range(GROUPS):
-                    acc_by_pos = project(m, codes_of[g], scales_of[g])
-                    nc.vector.scalar_tensor_tensor(
-                        out=positions_of_group(res[:], g),
-                        in0=acc_by_pos,
-                        scalar=gamma[:, m : m + 1],
-                        in1=positions_of_group(res[:], g),
-                        op0=ALU.mult,
-                        op1=ALU.add,
-                    )
-                nc.sync.dma_start(out=out_v[b, m], in_=res[:])
+        for b in range(B + 1):
+            for n in range(NH):
+                if b < B:
+                    sum_head(b, n)
+                    if n > 0:
+                        square_head(b, n - 1)
+                if b > 0:
+                    if n == 0:
+                        scale_factors(b - 1)
+                    quantise_chunk(b - 1, n)
+                    if n > 0:
+                        finish_chunk(b - 1, n - 1)
+            if b < B:
+                square_head(b, NH - 1)
+            if b > 0:
+                finish_chunk(b - 1, CHUNKS - 1)

@@ -18,54 +18,44 @@ NH = 4
 HEAD = 128
 HD = NH * HEAD
 POS = 32 * 64
+CHUNK = 512
+CHUNKS = POS // CHUNK
+QUAD = CHUNK // P
 HALVES = 2
 HALF = POS // HALVES
-OCT = HALF // P
-CHUNK = 512
-QUAD = CHUNK // P
-PAIR = OCT // QUAD
-CHUNKS = POS // CHUNK
+PAIR = CHUNKS // HALVES
 OT = HD // P
-VECTOR_TILES = (0, 2)
-SCALAR_TILES = (1, 3)
-R_PAD = 32
+HEADS = B * NH
 PREFETCH = 4
+LAG = 2
 EPS = 1e-8
 
 FLOPS = 2 * B * HD * HD * POS
 
-assert CHUNKS == NH
-
 
 def tile_axialattentionblock_pb_t_kernel(tc, xx, xy, x, norm2_w, out_w, out_b, gamma_att, out):
     nc = tc.nc
-    by_partition = "b n (hh hp) (wp i) c -> b n (hp wp) hh i c"
-    xx_v = xx.rearrange(by_partition, hh=HALVES, i=OCT)
-    xy_v = xy.rearrange(by_partition, hh=HALVES, i=OCT)
+    by_partition = "b n (g hp) (wp i) c -> b n (hp wp) g i c"
+    xx_v = xx.rearrange(by_partition, g=CHUNKS, i=QUAD)
+    xy_v = xy.rearrange(by_partition, g=CHUNKS, i=QUAD)
     x_v = x.rearrange("b (m p) h w -> b m p (h w)", p=P)
     out_v = out.rearrange("b (m p) h w -> b m p (h w)", p=P)
 
     with ExitStack() as ctx:
         const = ctx.enter_context(tc.tile_pool(name="const", bufs=1))
         stream = ctx.enter_context(tc.tile_pool(name="stream", bufs=PREFETCH))
-        xpool = ctx.enter_context(tc.tile_pool(name="xpool", bufs=B * OT))
+        xpool = ctx.enter_context(tc.tile_pool(name="xpool", bufs=3))
         respool = ctx.enter_context(tc.tile_pool(name="respool", bufs=1))
-        ypool = ctx.enter_context(tc.tile_pool(name="ypool", bufs=4))
         sums_pool = ctx.enter_context(tc.tile_pool(name="sums", bufs=2))
         big = ctx.enter_context(tc.tile_pool(name="big", bufs=2))
         junk = ctx.enter_context(tc.tile_pool(name="junk", bufs=1))
         work = ctx.enter_context(tc.tile_pool(name="work", bufs=3))
-        psum_t = ctx.enter_context(tc.psum_pool(name="psum_t", bufs=3))
+        psum_t = ctx.enter_context(tc.psum_pool(name="psum_t", bufs=4))
         psum_acc = ctx.enter_context(tc.psum_pool(name="psum_acc", bufs=4))
-        psum_r = ctx.enter_context(tc.psum_pool(name="psum_r", bufs=1))
-        ctx.enter_context(tc.manual_schedule())
+        pass
 
         ident = const.tile([P, P], BF16)
         make_identity(nc, ident[:])
-        ident32 = const.tile([P, P], F32)
-        make_identity(nc, ident32[:])
-        r_pad = const.tile([P, B, R_PAD], F32)
-        nc.vector.memset(r_pad[:], 0.0)
 
         one = const.tile([P, 1], F32)
         nc.vector.memset(one[:], 1.0)
@@ -84,10 +74,10 @@ def tile_axialattentionblock_pb_t_kernel(tc, xx, xy, x, norm2_w, out_w, out_b, g
 
         def load_head(u):
             b, n = divmod(u, NH)
-            xx_sb = stream.tile([P, HALVES, OCT, HEAD], BF16, tag="xx")
-            nc.sync.dma_start(out=xx_sb[:], in_=xx_v[b, n])
-            xy_sb = stream.tile([P, HALVES, OCT, HEAD], BF16, tag="xy")
-            nc.sync.dma_start(out=xy_sb[:], in_=xy_v[b, n])
+            xy_sb = stream.tile([P, CHUNKS * QUAD, HEAD], BF16, tag="xy")
+            nc.sync.dma_start(out=xy_sb[:].rearrange("p (g i) c -> p g i c", i=QUAD), in_=xy_v[b, n])
+            xx_sb = stream.tile([P, CHUNKS * QUAD, HEAD], BF16, tag="xx")
+            nc.sync.dma_start(out=xx_sb[:].rearrange("p (g i) c -> p g i c", i=QUAD), in_=xx_v[b, n])
             streams_of[u] = (xx_sb, xy_sb)
 
         for u in range(PREFETCH):
@@ -119,14 +109,14 @@ def tile_axialattentionblock_pb_t_kernel(tc, xx, xy, x, norm2_w, out_w, out_b, g
 
         sT_of = {}
         sums_of = {}
-        x_of = {}
-        res_of = {}
+        var_of = {}
         r_of = {}
+        res_of = {}
+        scaled_of = {}
         codes_of = {}
-        y_of = {}
 
-        def sum_head(b, n):
-            u = b * NH + n
+        def sum_head(u):
+            b, n = divmod(u, NH)
             if n == 0:
                 sT_of[b] = big.tile([P, NH, POS], F32, tag="sT", name="sT%d" % b)
                 sums_of[b] = (
@@ -134,13 +124,14 @@ def tile_axialattentionblock_pb_t_kernel(tc, xx, xy, x, norm2_w, out_w, out_b, g
                     sums_pool.tile([P, NH], F32, tag="sumsq", name="sumsq%d" % b),
                 )
             xx_sb, xy_sb = streams_of[u]
+            tiles = PAIR * QUAD
             for h in range(HALVES):
-                xyT = psum_t.tile([P, OCT, P], BF16, tag="tr")
-                for i in range(OCT):
-                    nc.tensor.transpose(xyT[:, i, :], xy_sb[:, h, i, :], ident[:])
-                xxT = psum_t.tile([P, OCT, P], BF16, tag="tr")
-                for i in range(OCT):
-                    nc.tensor.transpose(xxT[:, i, :], xx_sb[:, h, i, :], ident[:])
+                xyT = psum_t.tile([P, tiles, P], BF16, tag="tr")
+                for i in range(tiles):
+                    nc.tensor.transpose(xyT[:, i, :], xy_sb[:, h * tiles + i, :], ident[:])
+                xxT = psum_t.tile([P, tiles, P], BF16, tag="tr")
+                for i in range(tiles):
+                    nc.tensor.transpose(xxT[:, i, :], xx_sb[:, h * tiles + i, :], ident[:])
                 xyT_sb = work.tile([P, HALF], BF16, tag="xyT_sb")
                 nc.scalar.copy(out=xyT_sb[:], in_=xyT[:].rearrange("c i p -> c (i p)"))
                 nc.vector.scalar_tensor_tensor(
@@ -152,26 +143,25 @@ def tile_axialattentionblock_pb_t_kernel(tc, xx, xy, x, norm2_w, out_w, out_b, g
                     op1=ALU.add,
                     accum_out=sums_of[b][0][:, n, h : h + 1],
                 )
-            if u + PREFETCH < B * NH:
+            if u + PREFETCH < HEADS:
                 load_head(u + PREFETCH)
             m = n
             x_sb = xpool.tile([P, POS], BF16, tag="x")
             nc.sync.dma_start(out=x_sb[:], in_=x_v[b, m])
-            x_of[(b, m)] = x_sb
-            if m in VECTOR_TILES:
-                res = respool.tile([P, POS], F32, name="res%d%d" % (b, m))
-                nc.gpsimd.tensor_scalar(
-                    out=res[:], in0=x_sb[:], scalar1=1.0, scalar2=bias_gamma[:, m : m + 1], op0=ALU.mult, op1=ALU.add
-                )
-                res_of[(b, m)] = res
+            res = respool.tile([P, POS], F32, name="res%d%d" % (b, m))
+            nc.gpsimd.tensor_scalar(
+                out=res[:], in0=x_sb[:], scalar1=1.0, scalar2=bias_gamma[:, m : m + 1], op0=ALU.mult, op1=ALU.add
+            )
+            res_of[(b, m)] = res
 
-        def square_head(b, n):
+        def square_head(u):
+            b, n = divmod(u, NH)
             squares = junk.tile([P, POS], BF16, tag="squares")
             nc.scalar.activation(
                 out=squares[:], in_=sT_of[b][:, n, :], func=ACT.Square, accum_out=sums_of[b][1][:, n : n + 1]
             )
 
-        def scale_factors(b):
+        def deviation(b):
             sums, sumsq = sums_of[b]
             sum_s = sums_pool.tile([P, NH], F32, tag="sum_s")
             nc.vector.tensor_reduce(out=sum_s[:], in_=sums[:], axis=AX.X, op=ALU.add)
@@ -187,22 +177,35 @@ def tile_axialattentionblock_pb_t_kernel(tc, xx, xy, x, norm2_w, out_w, out_b, g
             )
             std = sums_pool.tile([P, NH], F32, tag="std")
             nc.scalar.activation(out=std[:], in_=var[:], func=ACT.Sqrt)
+            var_of[b] = std
+
+        def scale_factors(b):
             den = sums_pool.tile([P, NH], F32, tag="den")
-            nc.vector.tensor_scalar_add(out=den[:], in0=std[:], scalar1=EPS)
+            nc.vector.tensor_scalar_add(out=den[:], in0=var_of[b][:], scalar1=EPS)
             inv = sums_pool.tile([P, NH], F32, tag="inv")
             nc.vector.reciprocal(out=inv[:], in_=den[:])
-            nc.vector.tensor_tensor(out=r_pad[:, b, 0:NH], in0=inv[:], in1=half_w[:], op=ALU.mult)
-            r_ps = psum_r.tile([P, R_PAD], F32, tag="r")
-            nc.tensor.matmul(out=r_ps[:], lhsT=ident32[:], rhs=r_pad[:, b, :], start=True, stop=True)
-            r_of[b] = r_ps
+            r = sums_pool.tile([P, NH], F32, tag="r")
+            nc.vector.tensor_tensor(out=r[:], in0=inv[:], in1=half_w[:], op=ALU.mult)
+            r_of[b] = r
+
+        def scale_half(b, h):
+            scaled = work.tile([P, NH, HALF], BF16, tag="scaled", bufs=2)
+            for n in range(NH):
+                s_half = sT_of[b][:, n, h * HALF : (h + 1) * HALF]
+                if n % 2 == 0:
+                    nc.scalar.activation(out=scaled[:, n, :], in_=s_half, func=ACT.Copy, scale=r_of[b][:, n : n + 1])
+                else:
+                    nc.gpsimd.tensor_scalar(
+                        out=scaled[:, n, :], in0=s_half, scalar1=r_of[b][:, n : n + 1], scalar2=0.0, op0=ALU.mult, op1=ALU.add
+                    )
+            scaled_of[(b, h)] = scaled
 
         def quantise_chunk(b, g):
+            h, k = divmod(g, PAIR)
             grouped = work.tile([P, CHUNK, NH], BF16, tag="grouped", align_bytes=64)
-            nc.vector.tensor_tensor(
-                out=grouped[:],
-                in0=sT_of[b][:, :, g * CHUNK : (g + 1) * CHUNK].rearrange("c n p -> c p n"),
-                in1=r_of[b][:, 0:NH].unsqueeze(1).to_broadcast([P, CHUNK, NH]),
-                op=ALU.mult,
+            nc.vector.tensor_copy(
+                out=grouped[:].rearrange("c (q i) n -> c q n i", i=4),
+                in_=scaled_of[(b, h)][:, :, k * CHUNK : (k + 1) * CHUNK].rearrange("c n (q i) -> c q n i", i=4),
             )
             g_codes = work.tile([P, CHUNK], U32, tag="g_codes", align_bytes=64)
             g_scales = work.tile([P, CHUNK], U8, tag="g_scales", align_bytes=64)
@@ -213,15 +216,11 @@ def tile_axialattentionblock_pb_t_kernel(tc, xx, xy, x, norm2_w, out_w, out_b, g
             )
             codes_of[(b, g)] = (g_codes, g_scales)
 
-        def runs_of_chunk(half_ap, k):
-            return half_ap.rearrange("o (p k i) -> o p k i", k=PAIR, i=QUAD)[:, :, k, :]
-
         def finish_chunk(b, g):
-            h, k = divmod(g, PAIR)
-            half = slice(h * HALF, (h + 1) * HALF)
+            cols = slice(g * CHUNK, (g + 1) * CHUNK)
             g_codes, g_scales = codes_of[(b, g)]
             acc_of = {}
-            for m in SCALAR_TILES + VECTOR_TILES:
+            for m in range(OT):
                 acc = psum_acc.tile([P, CHUNK], F32, tag="acc")
                 nc.tensor.matmul_mx(
                     out=acc[:],
@@ -232,47 +231,33 @@ def tile_axialattentionblock_pb_t_kernel(tc, xx, xy, x, norm2_w, out_w, out_b, g
                     start=True,
                     stop=True,
                 )
-                acc_of[m] = acc[:].rearrange("o (i p) -> o p i", i=QUAD)
-            for m in SCALAR_TILES:
-                if k == 0:
-                    y_of[(b, m)] = ypool.tile([P, HALF], F32, tag="y", name="y%d%d%d" % (b, m, h))
-                y = y_of[(b, m)]
-                nc.scalar.activation(
-                    out=runs_of_chunk(y[:], k),
-                    in_=acc_of[m],
-                    func=ACT.Identity,
-                    bias=bias_gamma[:, m : m + 1],
-                    scale=gamma[:, m : m + 1],
-                )
-                if k == PAIR - 1:
-                    nc.gpsimd.tensor_tensor(out=y[:], in0=y[:], in1=x_of[(b, m)][:, half], op=ALU.add)
-                    nc.sync.dma_start(out=out_v[b, m][:, half], in_=y[:])
-            for m in VECTOR_TILES:
-                res = res_of[(b, m)]
+                acc_of[m] = acc
+            for m in range(OT):
+                res = res_of[(b, m)][:, cols].rearrange("o (p i) -> o p i", i=QUAD)
                 nc.vector.scalar_tensor_tensor(
-                    out=runs_of_chunk(res[:, half], k),
-                    in0=acc_of[m],
+                    out=res,
+                    in0=acc_of[m][:].rearrange("o (i p) -> o p i", i=QUAD),
                     scalar=gamma[:, m : m + 1],
-                    in1=runs_of_chunk(res[:, half], k),
+                    in1=res,
                     op0=ALU.mult,
                     op1=ALU.add,
                 )
-                if k == PAIR - 1:
-                    nc.sync.dma_start(out=out_v[b, m][:, half], in_=res[:, half])
+                nc.sync.dma_start(out=out_v[b, m][:, cols], in_=res_of[(b, m)][:, cols])
 
-        for b in range(B + 1):
-            for n in range(NH):
-                if b < B:
-                    sum_head(b, n)
-                    if n > 0:
-                        square_head(b, n - 1)
-                if b > 0:
-                    if n == 0:
-                        scale_factors(b - 1)
-                    quantise_chunk(b - 1, n)
-                    if n > 0:
-                        finish_chunk(b - 1, n - 1)
-            if b < B:
-                square_head(b, NH - 1)
-            if b > 0:
-                finish_chunk(b - 1, CHUNKS - 1)
+        for s in range(HEADS + NH + LAG + 1):
+            if s < HEADS:
+                sum_head(s)
+            if 0 < s <= HEADS:
+                square_head(s - 1)
+            if s % NH == 1 and NH < s <= HEADS + 1:
+                scale_factors(s // NH - 1)
+            ahead = s - NH - LAG + 1
+            if 0 <= ahead < B * CHUNKS and ahead % PAIR == 0:
+                scale_half(ahead // CHUNKS, (ahead % CHUNKS) // PAIR)
+            chunk = s - NH - LAG
+            if 0 <= chunk < B * CHUNKS:
+                quantise_chunk(chunk // CHUNKS, chunk % CHUNKS)
+            if 0 < chunk <= B * CHUNKS:
+                finish_chunk((chunk - 1) // CHUNKS, (chunk - 1) % CHUNKS)
+            if s % NH == 0 and s > 0 and s <= HEADS:
+                deviation(s // NH - 1)

@@ -24,6 +24,9 @@ QUAD = CHUNK // P
 HALVES = 2
 HALF = POS // HALVES
 PAIR = CHUNKS // HALVES
+BANK_TILES = 4
+RUN = BANK_TILES * P
+RUNS = POS // RUN
 OT = HD // P
 HEADS = B * NH
 PREFETCH = 4
@@ -50,9 +53,7 @@ def tile_axialattentionblock_pb_t_kernel(tc, xx, xy, x, norm2_w, out_w, out_b, g
         big = ctx.enter_context(tc.tile_pool(name="big", bufs=2))
         junk = ctx.enter_context(tc.tile_pool(name="junk", bufs=1))
         work = ctx.enter_context(tc.tile_pool(name="work", bufs=3))
-        psum_t = ctx.enter_context(tc.psum_pool(name="psum_t", bufs=4))
-        psum_acc = ctx.enter_context(tc.psum_pool(name="psum_acc", bufs=4))
-        pass
+        psum = ctx.enter_context(tc.psum_pool(name="psum", bufs=8))
 
         ident = const.tile([P, P], BF16)
         make_identity(nc, ident[:])
@@ -68,7 +69,6 @@ def tile_axialattentionblock_pb_t_kernel(tc, xx, xy, x, norm2_w, out_w, out_b, g
         nc.sync.dma_start(out=vec_rows[NH : 2 * NH, :], in_=out_b.rearrange("(n c) -> n c", c=HEAD))
         nc.sync.dma_start(out=vec_rows[2 * NH : 3 * NH, :], in_=gamma_att.rearrange("(n c) -> n c", c=HEAD))
         w_rows = const.tile([P, OT, HD], BF16)
-        nc.sync.dma_start(out=w_rows[:], in_=out_w.rearrange("(m p) j -> p m j", p=P))
 
         streams_of = {}
 
@@ -80,10 +80,12 @@ def tile_axialattentionblock_pb_t_kernel(tc, xx, xy, x, norm2_w, out_w, out_b, g
             nc.sync.dma_start(out=xx_sb[:].rearrange("p (g i) c -> p g i c", i=QUAD), in_=xx_v[b, n])
             streams_of[u] = (xx_sb, xy_sb)
 
-        for u in range(PREFETCH):
+        load_head(0)
+        nc.sync.dma_start(out=w_rows[:], in_=out_w.rearrange("(m p) j -> p m j", p=P))
+        for u in range(1, PREFETCH):
             load_head(u)
 
-        vec_ps = psum_t.tile([P, P], BF16, tag="tr")
+        vec_ps = psum.tile([P, P], BF16, tag="bank")
         nc.tensor.transpose(vec_ps[:], vec_rows[:], ident[:])
         vecs = const.tile([P, 3 * NH], F32)
         nc.vector.tensor_copy(out=vecs[:], in_=vec_ps[:, 0 : 3 * NH])
@@ -94,18 +96,20 @@ def tile_axialattentionblock_pb_t_kernel(tc, xx, xy, x, norm2_w, out_w, out_b, g
         nc.vector.tensor_tensor(out=bias_gamma[:], in0=vecs[:, NH : 2 * NH], in1=gamma, op=ALU.mult)
 
         w_grouped = const.tile([P, OT, P, NH], BF16, align_bytes=64)
-        for m in range(OT):
-            wT = psum_t.tile([P, NH, P], BF16, tag="tr")
-            for t in range(NH):
-                nc.tensor.transpose(wT[:, t, :], w_rows[:, m, t * HEAD : (t + 1) * HEAD], ident[:])
-            nc.vector.tensor_copy(out=w_grouped[:, m], in_=wT[:].rearrange("k t o -> k o t"))
         w_codes = const.tile([P, HD], U32, align_bytes=64)
         w_scales = const.tile([P, HD], U8, align_bytes=64)
-        nc.vector.quantize_mx(
-            out=w_codes[:].bitcast(FP8X4),
-            scales=w_scales[:],
-            in_=w_grouped[:].rearrange("k m o t -> k (m o t)"),
-        )
+
+        def quantise_weights():
+            for m in range(OT):
+                wT = psum.tile([P, NH, P], BF16, tag="bank")
+                for t in range(NH):
+                    nc.tensor.transpose(wT[:, t, :], w_rows[:, m, t * HEAD : (t + 1) * HEAD], ident[:])
+                nc.vector.tensor_copy(out=w_grouped[:, m], in_=wT[:].rearrange("k t o -> k o t"))
+            nc.vector.quantize_mx(
+                out=w_codes[:].bitcast(FP8X4),
+                scales=w_scales[:],
+                in_=w_grouped[:].rearrange("k m o t -> k (m o t)"),
+            )
 
         sT_of = {}
         sums_of = {}
@@ -120,32 +124,32 @@ def tile_axialattentionblock_pb_t_kernel(tc, xx, xy, x, norm2_w, out_w, out_b, g
             if n == 0:
                 sT_of[b] = big.tile([P, NH, POS], F32, tag="sT", name="sT%d" % b)
                 sums_of[b] = (
-                    sums_pool.tile([P, NH, HALVES], F32, tag="sums", name="sums%d" % b),
+                    sums_pool.tile([P, NH, RUNS], F32, tag="sums", name="sums%d" % b),
                     sums_pool.tile([P, NH], F32, tag="sumsq", name="sumsq%d" % b),
                 )
             xx_sb, xy_sb = streams_of[u]
-            tiles = PAIR * QUAD
-            for h in range(HALVES):
-                xyT = psum_t.tile([P, tiles, P], BF16, tag="tr")
-                for i in range(tiles):
-                    nc.tensor.transpose(xyT[:, i, :], xy_sb[:, h * tiles + i, :], ident[:])
-                xxT = psum_t.tile([P, tiles, P], BF16, tag="tr")
-                for i in range(tiles):
-                    nc.tensor.transpose(xxT[:, i, :], xx_sb[:, h * tiles + i, :], ident[:])
-                xyT_sb = work.tile([P, HALF], BF16, tag="xyT_sb")
+            for k in range(RUNS):
+                xyT = psum.tile([P, BANK_TILES, P], BF16, tag="bank")
+                for i in range(BANK_TILES):
+                    nc.tensor.transpose(xyT[:, i, :], xy_sb[:, k * BANK_TILES + i, :], ident[:])
+                xxT = psum.tile([P, BANK_TILES, P], BF16, tag="bank")
+                for i in range(BANK_TILES):
+                    nc.tensor.transpose(xxT[:, i, :], xx_sb[:, k * BANK_TILES + i, :], ident[:])
+                xyT_sb = work.tile([P, RUN], BF16, tag="xyT_sb")
                 nc.scalar.copy(out=xyT_sb[:], in_=xyT[:].rearrange("c i p -> c (i p)"))
                 nc.vector.scalar_tensor_tensor(
-                    out=sT_of[b][:, n, h * HALF : (h + 1) * HALF],
+                    out=sT_of[b][:, n, k * RUN : (k + 1) * RUN],
                     in0=xxT[:].rearrange("c i p -> c (i p)"),
                     scalar=1.0,
                     in1=xyT_sb[:],
                     op0=ALU.mult,
                     op1=ALU.add,
-                    accum_out=sums_of[b][0][:, n, h : h + 1],
+                    accum_out=sums_of[b][0][:, n, k : k + 1],
                 )
             if u + PREFETCH < HEADS:
                 load_head(u + PREFETCH)
-            m = n
+
+        def residual_tile(b, m):
             x_sb = xpool.tile([P, POS], BF16, tag="x")
             nc.sync.dma_start(out=x_sb[:], in_=x_v[b, m])
             res = respool.tile([P, POS], F32, name="res%d%d" % (b, m))
@@ -221,7 +225,7 @@ def tile_axialattentionblock_pb_t_kernel(tc, xx, xy, x, norm2_w, out_w, out_b, g
             g_codes, g_scales = codes_of[(b, g)]
             acc_of = {}
             for m in range(OT):
-                acc = psum_acc.tile([P, CHUNK], F32, tag="acc")
+                acc = psum.tile([P, CHUNK], F32, tag="bank")
                 nc.tensor.matmul_mx(
                     out=acc[:],
                     lhsT=w_codes[:, m * P : (m + 1) * P].bitcast(FP8X4),
@@ -247,6 +251,10 @@ def tile_axialattentionblock_pb_t_kernel(tc, xx, xy, x, norm2_w, out_w, out_b, g
         for s in range(HEADS + NH + LAG + 1):
             if s < HEADS:
                 sum_head(s)
+            if 0 <= s - NH < B * OT:
+                residual_tile((s - NH) // OT, (s - NH) % OT)
+            if s == 1:
+                quantise_weights()
             if 0 < s <= HEADS:
                 square_head(s - 1)
             if s % NH == 1 and NH < s <= HEADS + 1:

@@ -28,6 +28,8 @@ BANK_TILES = 4
 RUN = BANK_TILES * P
 RUNS = POS // RUN
 OT = HD // P
+VECTOR_TILES = (0, 2)
+SCALAR_TILES = (1, 3)
 HEADS = B * NH
 PREFETCH = 4
 LAG = 2
@@ -47,7 +49,9 @@ def tile_axialattentionblock_pb_t_kernel(tc, xx, xy, x, norm2_w, out_w, out_b, g
     with ExitStack() as ctx:
         const = ctx.enter_context(tc.tile_pool(name="const", bufs=1))
         stream = ctx.enter_context(tc.tile_pool(name="stream", bufs=PREFETCH))
-        xpool = ctx.enter_context(tc.tile_pool(name="xpool", bufs=3))
+        xpool = ctx.enter_context(tc.tile_pool(name="xpool", bufs=2))
+        xkeep = ctx.enter_context(tc.tile_pool(name="xkeep", bufs=B * len(SCALAR_TILES)))
+        ypool = ctx.enter_context(tc.tile_pool(name="ypool", bufs=4))
         respool = ctx.enter_context(tc.tile_pool(name="respool", bufs=1))
         sums_pool = ctx.enter_context(tc.tile_pool(name="sums", bufs=2))
         big = ctx.enter_context(tc.tile_pool(name="big", bufs=2))
@@ -116,6 +120,7 @@ def tile_axialattentionblock_pb_t_kernel(tc, xx, xy, x, norm2_w, out_w, out_b, g
         var_of = {}
         r_of = {}
         res_of = {}
+        x_of = {}
         scaled_of = {}
         codes_of = {}
 
@@ -150,13 +155,18 @@ def tile_axialattentionblock_pb_t_kernel(tc, xx, xy, x, norm2_w, out_w, out_b, g
                 load_head(u + PREFETCH)
 
         def residual_tile(b, m):
-            x_sb = xpool.tile([P, POS], BF16, tag="x")
-            nc.sync.dma_start(out=x_sb[:], in_=x_v[b, m])
-            res = respool.tile([P, POS], F32, name="res%d%d" % (b, m))
-            nc.gpsimd.tensor_scalar(
-                out=res[:], in0=x_sb[:], scalar1=1.0, scalar2=bias_gamma[:, m : m + 1], op0=ALU.mult, op1=ALU.add
-            )
-            res_of[(b, m)] = res
+            if m in SCALAR_TILES:
+                x_sb = xkeep.tile([P, POS], BF16, tag="x_kept")
+                nc.sync.dma_start(out=x_sb[:], in_=x_v[b, m])
+                x_of[(b, m)] = x_sb
+            else:
+                x_sb = xpool.tile([P, POS], BF16, tag="x")
+                nc.sync.dma_start(out=x_sb[:], in_=x_v[b, m])
+                res = respool.tile([P, POS], F32, name="res%d%d" % (b, m))
+                nc.gpsimd.tensor_scalar(
+                    out=res[:], in0=x_sb[:], scalar1=1.0, scalar2=bias_gamma[:, m : m + 1], op0=ALU.mult, op1=ALU.add
+                )
+                res_of[(b, m)] = res
 
         def square_head(u):
             b, n = divmod(u, NH)
@@ -224,7 +234,7 @@ def tile_axialattentionblock_pb_t_kernel(tc, xx, xy, x, norm2_w, out_w, out_b, g
             cols = slice(g * CHUNK, (g + 1) * CHUNK)
             g_codes, g_scales = codes_of[(b, g)]
             acc_of = {}
-            for m in range(OT):
+            for m in SCALAR_TILES + VECTOR_TILES:
                 acc = psum.tile([P, CHUNK], F32, tag="bank")
                 nc.tensor.matmul_mx(
                     out=acc[:],
@@ -235,12 +245,23 @@ def tile_axialattentionblock_pb_t_kernel(tc, xx, xy, x, norm2_w, out_w, out_b, g
                     start=True,
                     stop=True,
                 )
-                acc_of[m] = acc
-            for m in range(OT):
+                acc_of[m] = acc[:].rearrange("o (i p) -> o p i", i=QUAD)
+            for m in SCALAR_TILES:
+                y = ypool.tile([P, CHUNK], F32, tag="y")
+                nc.scalar.activation(
+                    out=y[:].rearrange("o (p i) -> o p i", i=QUAD),
+                    in_=acc_of[m],
+                    func=ACT.Identity,
+                    bias=bias_gamma[:, m : m + 1],
+                    scale=gamma[:, m : m + 1],
+                )
+                nc.gpsimd.tensor_tensor(out=y[:], in0=y[:], in1=x_of[(b, m)][:, cols], op=ALU.add)
+                nc.sync.dma_start(out=out_v[b, m][:, cols], in_=y[:])
+            for m in VECTOR_TILES:
                 res = res_of[(b, m)][:, cols].rearrange("o (p i) -> o p i", i=QUAD)
                 nc.vector.scalar_tensor_tensor(
                     out=res,
-                    in0=acc_of[m][:].rearrange("o (i p) -> o p i", i=QUAD),
+                    in0=acc_of[m],
                     scalar=gamma[:, m : m + 1],
                     in1=res,
                     op0=ALU.mult,

from contextlib import ExitStack

import concourse.mybir as mybir
from concourse.masks import make_identity

F32 = mybir.dt.float32
BF16 = mybir.dt.bfloat16
U32 = mybir.dt.uint32
U8 = mybir.dt.uint8
FP8X4 = mybir.dt.float8_e4m3fn_x4
ALU = mybir.AluOpType
ACT = mybir.ActivationFunctionType
AX = mybir.AxisListType

P = 128
B = 2
NH = 4
HEAD = 128
HD = NH * HEAD
POS = 32 * 64
CHUNK = 512
CHUNKS = POS // CHUNK
QUAD = CHUNK // P
HALVES = 2
HALF = POS // HALVES
PAIR = CHUNKS // HALVES
BANK_TILES = 4
RUN = BANK_TILES * P
RUNS = POS // RUN
OT = HD // P
VECTOR_TILES = (0, 2)
SCALAR_TILES = (1, 3)
HEADS = B * NH
PREFETCH = 4
LAG = 2
EPS = 1e-8

FLOPS = 2 * B * HD * HD * POS


def tile_axialattentionblock_pb_t_kernel(tc, xx, xy, x, norm2_w, out_w, out_b, gamma_att, out):
    nc = tc.nc
    by_partition = "b n (g hp) (wp i) c -> b n (hp wp) g i c"
    xx_v = xx.rearrange(by_partition, g=CHUNKS, i=QUAD)
    xy_v = xy.rearrange(by_partition, g=CHUNKS, i=QUAD)
    x_v = x.rearrange("b (m p) h w -> b m p (h w)", p=P)
    out_v = out.rearrange("b (m p) h w -> b m p (h w)", p=P)

    with ExitStack() as ctx:
        const = ctx.enter_context(tc.tile_pool(name="const", bufs=1))
        stream = ctx.enter_context(tc.tile_pool(name="stream", bufs=PREFETCH))
        xpool = ctx.enter_context(tc.tile_pool(name="xpool", bufs=2))
        xkeep = ctx.enter_context(tc.tile_pool(name="xkeep", bufs=B * len(SCALAR_TILES)))
        ypool = ctx.enter_context(tc.tile_pool(name="ypool", bufs=4))
        respool = ctx.enter_context(tc.tile_pool(name="respool", bufs=1))
        sums_pool = ctx.enter_context(tc.tile_pool(name="sums", bufs=2))
        big = ctx.enter_context(tc.tile_pool(name="big", bufs=2))
        junk = ctx.enter_context(tc.tile_pool(name="junk", bufs=1))
        work = ctx.enter_context(tc.tile_pool(name="work", bufs=3))
        psum = ctx.enter_context(tc.psum_pool(name="psum", bufs=8))

        ident = const.tile([P, P], BF16)
        make_identity(nc, ident[:])

        one = const.tile([P, 1], F32)
        nc.vector.memset(one[:], 1.0)
        one_root = const.tile([P, 1], F32)
        nc.scalar.activation(out=one_root[:], in_=one[:], func=ACT.Sqrt)

        vec_rows = const.tile([P, P], BF16)
        nc.vector.memset(vec_rows[:], 0.0)
        nc.sync.dma_start(out=vec_rows[0:NH, :], in_=norm2_w.rearrange("(n c) -> n c", c=HEAD))
        nc.sync.dma_start(out=vec_rows[NH : 2 * NH, :], in_=out_b.rearrange("(n c) -> n c", c=HEAD))
        nc.sync.dma_start(out=vec_rows[2 * NH : 3 * NH, :], in_=gamma_att.rearrange("(n c) -> n c", c=HEAD))
        w_rows = const.tile([P, OT, HD], BF16)

        streams_of = {}

        def load_head(u):
            b, n = divmod(u, NH)
            xy_sb = stream.tile([P, CHUNKS * QUAD, HEAD], BF16, tag="xy")
            nc.sync.dma_start(out=xy_sb[:].rearrange("p (g i) c -> p g i c", i=QUAD), in_=xy_v[b, n])
            xx_sb = stream.tile([P, CHUNKS * QUAD, HEAD], BF16, tag="xx")
            nc.sync.dma_start(out=xx_sb[:].rearrange("p (g i) c -> p g i c", i=QUAD), in_=xx_v[b, n])
            streams_of[u] = (xx_sb, xy_sb)

        load_head(0)
        nc.sync.dma_start(out=w_rows[:], in_=out_w.rearrange("(m p) j -> p m j", p=P))
        for u in range(1, PREFETCH):
            load_head(u)

        vec_ps = psum.tile([P, P], BF16, tag="bank")
        nc.tensor.transpose(vec_ps[:], vec_rows[:], ident[:])
        vecs = const.tile([P, 3 * NH], F32)
        nc.vector.tensor_copy(out=vecs[:], in_=vec_ps[:, 0 : 3 * NH])
        gamma = vecs[:, 2 * NH : 3 * NH]
        half_w = const.tile([P, NH], F32)
        nc.vector.tensor_scalar_mul(out=half_w[:], in0=vecs[:, 0:NH], scalar1=0.5)
        bias_gamma = const.tile([P, OT], F32)
        nc.vector.tensor_tensor(out=bias_gamma[:], in0=vecs[:, NH : 2 * NH], in1=gamma, op=ALU.mult)

        w_grouped = const.tile([P, OT, P, NH], BF16, align_bytes=64)
        w_codes = const.tile([P, HD], U32, align_bytes=64)
        w_scales = const.tile([P, HD], U8, align_bytes=64)

        def quantise_weights():
            for m in range(OT):
                wT = psum.tile([P, NH, P], BF16, tag="bank")
                for t in range(NH):
                    nc.tensor.transpose(wT[:, t, :], w_rows[:, m, t * HEAD : (t + 1) * HEAD], ident[:])
                nc.vector.tensor_copy(out=w_grouped[:, m], in_=wT[:].rearrange("k t o -> k o t"))
            nc.vector.quantize_mx(
                out=w_codes[:].bitcast(FP8X4),
                scales=w_scales[:],
                in_=w_grouped[:].rearrange("k m o t -> k (m o t)"),
            )

        sT_of = {}
        sums_of = {}
        var_of = {}
        r_of = {}
        res_of = {}
        x_of = {}
        scaled_of = {}
        codes_of = {}

        def sum_head(u):
            b, n = divmod(u, NH)
            if n == 0:
                sT_of[b] = big.tile([P, NH, POS], F32, tag="sT", name="sT%d" % b)
                sums_of[b] = (
                    sums_pool.tile([P, NH, RUNS], F32, tag="sums", name="sums%d" % b),
                    sums_pool.tile([P, NH], F32, tag="sumsq", name="sumsq%d" % b),
                )
            xx_sb, xy_sb = streams_of[u]
            for k in range(RUNS):
                xyT = psum.tile([P, BANK_TILES, P], BF16, tag="bank")
                for i in range(BANK_TILES):
                    nc.tensor.transpose(xyT[:, i, :], xy_sb[:, k * BANK_TILES + i, :], ident[:])
                xxT = psum.tile([P, BANK_TILES, P], BF16, tag="bank")
                for i in range(BANK_TILES):
                    nc.tensor.transpose(xxT[:, i, :], xx_sb[:, k * BANK_TILES + i, :], ident[:])
                xyT_sb = work.tile([P, RUN], BF16, tag="xyT_sb")
                nc.scalar.copy(out=xyT_sb[:], in_=xyT[:].rearrange("c i p -> c (i p)"))
                nc.vector.scalar_tensor_tensor(
                    out=sT_of[b][:, n, k * RUN : (k + 1) * RUN],
                    in0=xxT[:].rearrange("c i p -> c (i p)"),
                    scalar=1.0,
                    in1=xyT_sb[:],
                    op0=ALU.mult,
                    op1=ALU.add,
                    accum_out=sums_of[b][0][:, n, k : k + 1],
                )
            if u + PREFETCH < HEADS:
                load_head(u + PREFETCH)

        def residual_tile(b, m):
            if m in SCALAR_TILES:
                x_sb = xkeep.tile([P, POS], BF16, tag="x_kept")
                nc.sync.dma_start(out=x_sb[:], in_=x_v[b, m])
                x_of[(b, m)] = x_sb
            else:
                x_sb = xpool.tile([P, POS], BF16, tag="x")
                nc.sync.dma_start(out=x_sb[:], in_=x_v[b, m])
                res = respool.tile([P, POS], F32, name="res%d%d" % (b, m))
                nc.gpsimd.tensor_scalar(
                    out=res[:], in0=x_sb[:], scalar1=1.0, scalar2=bias_gamma[:, m : m + 1], op0=ALU.mult, op1=ALU.add
                )
                res_of[(b, m)] = res

        def square_head(u):
            b, n = divmod(u, NH)
            squares = junk.tile([P, POS], BF16, tag="squares")
            nc.scalar.activation(
                out=squares[:], in_=sT_of[b][:, n, :], func=ACT.Square, accum_out=sums_of[b][1][:, n : n + 1]
            )

        def deviation(b):
            sums, sumsq = sums_of[b]
            sum_s = sums_pool.tile([P, NH], F32, tag="sum_s")
            nc.vector.tensor_reduce(out=sum_s[:], in_=sums[:], axis=AX.X, op=ALU.add)
            sum_s2 = sums_pool.tile([P, NH], F32, tag="sum_s2")
            nc.vector.tensor_tensor(out=sum_s2[:], in0=sum_s[:], in1=sum_s[:], op=ALU.mult)
            centred = sums_pool.tile([P, NH], F32, tag="centred")
            nc.vector.scalar_tensor_tensor(
                out=centred[:], in0=sum_s2[:], scalar=-1.0 / POS, in1=sumsq[:], op0=ALU.mult, op1=ALU.add
            )
            var = sums_pool.tile([P, NH], F32, tag="var")
            nc.vector.tensor_scalar(
                out=var[:], in0=centred[:], scalar1=0.25 / (POS - 1), scalar2=0.0, op0=ALU.mult, op1=ALU.max
            )
            std = sums_pool.tile([P, NH], F32, tag="std")
            nc.scalar.activation(out=std[:], in_=var[:], func=ACT.Sqrt)
            var_of[b] = std

        def scale_factors(b):
            den = sums_pool.tile([P, NH], F32, tag="den")
            nc.vector.tensor_scalar_add(out=den[:], in0=var_of[b][:], scalar1=EPS)
            inv = sums_pool.tile([P, NH], F32, tag="inv")
            nc.vector.reciprocal(out=inv[:], in_=den[:])
            r = sums_pool.tile([P, NH], F32, tag="r")
            nc.vector.tensor_tensor(out=r[:], in0=inv[:], in1=half_w[:], op=ALU.mult)
            r_of[b] = r

        def scale_half(b, h):
            scaled = work.tile([P, NH, HALF], BF16, tag="scaled", bufs=2)
            for n in range(NH):
                s_half = sT_of[b][:, n, h * HALF : (h + 1) * HALF]
                if n % 2 == 0:
                    nc.scalar.activation(out=scaled[:, n, :], in_=s_half, func=ACT.Copy, scale=r_of[b][:, n : n + 1])
                else:
                    nc.gpsimd.tensor_scalar(
                        out=scaled[:, n, :], in0=s_half, scalar1=r_of[b][:, n : n + 1], scalar2=0.0, op0=ALU.mult, op1=ALU.add
                    )
            scaled_of[(b, h)] = scaled

        def quantise_chunk(b, g):
            h, k = divmod(g, PAIR)
            grouped = work.tile([P, CHUNK, NH], BF16, tag="grouped", align_bytes=64)
            nc.vector.tensor_copy(
                out=grouped[:].rearrange("c (q i) n -> c q n i", i=4),
                in_=scaled_of[(b, h)][:, :, k * CHUNK : (k + 1) * CHUNK].rearrange("c n (q i) -> c q n i", i=4),
            )
            g_codes = work.tile([P, CHUNK], U32, tag="g_codes", align_bytes=64)
            g_scales = work.tile([P, CHUNK], U8, tag="g_scales", align_bytes=64)
            nc.vector.quantize_mx(
                out=g_codes[:].bitcast(FP8X4),
                scales=g_scales[:],
                in_=grouped[:].rearrange("c p n -> c (p n)"),
            )
            codes_of[(b, g)] = (g_codes, g_scales)

        def finish_chunk(b, g):
            cols = slice(g * CHUNK, (g + 1) * CHUNK)
            g_codes, g_scales = codes_of[(b, g)]
            acc_of = {}
            for m in SCALAR_TILES + VECTOR_TILES:
                acc = psum.tile([P, CHUNK], F32, tag="bank")
                nc.tensor.matmul_mx(
                    out=acc[:],
                    lhsT=w_codes[:, m * P : (m + 1) * P].bitcast(FP8X4),
                    lhsT_scale=w_scales[:, m * P : (m + 1) * P],
                    rhs=g_codes[:].bitcast(FP8X4),
                    rhs_scale=g_scales[:],
                    start=True,
                    stop=True,
                )
                acc_of[m] = acc[:].rearrange("o (i p) -> o p i", i=QUAD)
            for m in SCALAR_TILES:
                y = ypool.tile([P, CHUNK], F32, tag="y")
                nc.scalar.activation(
                    out=y[:].rearrange("o (p i) -> o p i", i=QUAD),
                    in_=acc_of[m],
                    func=ACT.Identity,
                    bias=bias_gamma[:, m : m + 1],
                    scale=gamma[:, m : m + 1],
                )
                nc.gpsimd.tensor_tensor(out=y[:], in0=y[:], in1=x_of[(b, m)][:, cols], op=ALU.add)
                nc.sync.dma_start(out=out_v[b, m][:, cols], in_=y[:])
            for m in VECTOR_TILES:
                res = res_of[(b, m)][:, cols].rearrange("o (p i) -> o p i", i=QUAD)
                nc.vector.scalar_tensor_tensor(
                    out=res,
                    in0=acc_of[m],
                    scalar=gamma[:, m : m + 1],
                    in1=res,
                    op0=ALU.mult,
                    op1=ALU.add,
                )
                nc.sync.dma_start(out=out_v[b, m][:, cols], in_=res_of[(b, m)][:, cols])

        for s in range(HEADS + NH + LAG + 1):
            if s < HEADS:
                sum_head(s)
            if 0 <= s - NH < B * OT:
                residual_tile((s - NH) // OT, (s - NH) % OT)
            if s == 1:
                quantise_weights()
            if 0 < s <= HEADS:
                square_head(s - 1)
            if s % NH == 1 and NH < s <= HEADS + 1:
                scale_factors(s // NH - 1)
            ahead = s - NH - LAG + 1
            if 0 <= ahead < B * CHUNKS and ahead % PAIR == 0:
                scale_half(ahead // CHUNKS, (ahead % CHUNKS) // PAIR)
            chunk = s - NH - LAG
            if 0 <= chunk < B * CHUNKS:
                quantise_chunk(chunk // CHUNKS, chunk % CHUNKS)
            if 0 < chunk <= B * CHUNKS:
                finish_chunk((chunk - 1) // CHUNKS, (chunk - 1) % CHUNKS)
            if s % NH == 0 and s > 0 and s <= HEADS:
                deviation(s // NH - 1)
